import numpy as np
import ml_dtypes


def mxq(x, axis, fmt="e4m3"):
    dtype, down = {"e4m3": (ml_dtypes.float8_e4m3fn, 7), "e5m2": (ml_dtypes.float8_e5m2, 14)}[fmt]
    v = np.moveaxis(np.asarray(x, np.float32).astype(ml_dtypes.bfloat16).astype(np.float64), axis, -1)
    blocks = v.reshape(v.shape[:-1] + (-1, 32))
    amax = np.abs(blocks).max(-1, keepdims=True)
    byte = np.maximum(np.where(amax > 0, np.frexp(amax)[1] - 1 + 127, 0) - down, 1)
    scale = np.exp2(byte - 127.0)
    codes = (blocks / scale).astype(np.float32).astype(dtype).astype(np.float64)
    return np.moveaxis((codes * scale).reshape(v.shape), -1, axis)


WIDE = False


def mx_kscale(k):
    if not WIDE:
        return np.ones(k)
    levels = np.array([10, -10, 5, -5, 0])
    if k % 512:
        return np.exp2(np.random.permutation(np.resize(levels, k // 32))).repeat(32)
    a = np.empty((k // 512, 16))
    for p in range(k // 512):
        a[p, :8] = np.random.permutation(np.resize(levels, 8))
        for g in range(8):
            far = levels[np.abs(levels - a[p, g]) >= 10]
            a[p, g + 8] = far[np.random.randint(len(far))]
    return np.exp2(a.ravel()).repeat(32)


BF16 = ml_dtypes.bfloat16


def bf(x):
    return np.asarray(x, np.float32).astype(BF16)


def f64(x):
    return np.asarray(x).astype(np.float64)


N, C, K, M, HH, WW, CO = 4, 512, 512, 128, 32, 32, 512
P = HH * WW


def setup_inputs():
    s, t = mx_kscale(K), mx_kscale(K)
    return {"h_pix": bf(np.maximum(np.random.standard_normal((N, K, P)), 0.0) * 1.5 * s[None, :, None]),
            "wp2": bf(np.random.standard_normal((K, K)) * np.sqrt(2.0 / K) * t[:, None] / s[None, :]),
            "sp2": bf(np.random.uniform(0.5, 1.5, K)),
            "bp2": bf(np.random.standard_normal(K) * 0.2 * t),
            "key_obj": bf(np.maximum(np.random.standard_normal((N, K, M)), 0.0) * 1.5 / t[None, :, None])}


def reference(h_pix, wp2, sp2, bp2, key_obj):
    y = f64(bf(mxq(f64(wp2), 1, "e4m3") @ mxq(f64(h_pix), 1, "e4m3")))
    query = np.maximum(y * f64(sp2)[None, :, None] + f64(bp2)[None, :, None], 0.0)
    sim = (mxq(query, 1, "e4m3").transpose(0, 2, 1) @ mxq(f64(key_obj), 1, "e4m3")) * (K ** -0.5)
    e = np.exp(sim - sim.max(-1, keepdims=True))
    return e / e.sum(-1, keepdims=True)

@@ -1,0 +1,283 @@
+from contextlib import ExitStack
+
+import concourse.mybir as mybir
+from concourse.masks import make_identity
+
+F32 = mybir.dt.float32
+BF16 = mybir.dt.bfloat16
+U32 = mybir.dt.uint32
+U8 = mybir.dt.uint8
+FP8X4 = mybir.dt.float8_e4m3fn_x4
+ACT = mybir.ActivationFunctionType
+ALU = mybir.AluOpType
+AX = mybir.AxisListType
+
+IMAGES, CH, PIXELS, REGIONS = 4, 512, 1024, 128
+P = 128
+PACK = 4
+CHUNK = 512
+HALF = 256
+RUN = 4
+S_SHARE = 192
+PER_IMAGE = PIXELS // CHUNK
+CHUNKS = IMAGES * PER_IMAGE
+SUB = CHUNK // P
+SIM_SCALE = CH ** -0.5
+LEAD = 2
+BANK_DT = BF16
+Y_BUFS = 6
+UNITS = [(c, 0, SUB) for c in range(CHUNKS - 1)] + [(CHUNKS - 1, 0, 2), (CHUNKS - 1, 2, 4)]
+
+FLOPS = 2 * IMAGES * CH * CH * PIXELS + 2 * IMAGES * PIXELS * CH * REGIONS
+
+
+def tile_spatialocr_module_pa_kernel(tc, h_pix, wp2, sp2, bp2, key_obj, out):
+    nc = tc.nc
+    with ExitStack() as ctx:
+        const = ctx.enter_context(tc.tile_pool(name="const", bufs=1))
+        work = ctx.enter_context(tc.tile_pool(name="work", bufs=2))
+        psy = ctx.enter_context(tc.psum_pool(name="psy", bufs=Y_BUFS))
+        pss = ctx.enter_context(tc.psum_pool(name="pss", bufs=2))
+
+        h_view = {}
+
+        def load_h(c, split):
+            n, w0 = c // PER_IMAGE, (c % PER_IMAGE) * CHUNK
+            src = h_pix[n].rearrange("(p j) w -> p j w", j=PACK)
+            if split:
+                t_s = const.tile([P, PACK, S_SHARE], BF16, name="h%d_s" % c)
+                t_v = const.tile([P, PACK, CHUNK - S_SHARE], BF16, name="h%d_v" % c)
+                nc.sync.dma_start(out=t_v[:], in_=src[:, :, w0 + S_SHARE : w0 + CHUNK])
+                nc.sync.dma_start(out=t_s[:], in_=src[:, :, w0 : w0 + S_SHARE])
+                h_view[c] = [t_s[:], t_v[:]]
+            else:
+                t = const.tile([P, PACK, CHUNK], BF16, name="h%d" % c)
+                nc.sync.dma_start(out=t[:], in_=src[:, :, w0 : w0 + CHUNK])
+                h_view[c] = [t[:, :, 0:S_SHARE], t[:, :, S_SHARE:CHUNK]]
+
+        gain_raw = const.tile([P, PACK], BF16, name="gain_raw")
+        bias_raw = const.tile([P, PACK], BF16, name="bias_raw")
+        nc.scalar.dma_start(out=gain_raw[:], in_=sp2.rearrange("(p t) -> p t", t=PACK))
+        nc.scalar.dma_start(out=bias_raw[:], in_=bp2.rearrange("(p t) -> p t", t=PACK))
+        load_h(0, True)
+        w_sb = const.tile([P, PACK, CH], BF16, name="w_sb")
+        nc.sync.dma_start(out=w_sb[:], in_=wp2.rearrange("(m t) k -> m t k", t=PACK))
+        load_h(1, False)
+        k_raw = const.tile([P, IMAGES, PACK, REGIONS], BF16, name="k_raw")
+        nc.sync.dma_start(
+            out=k_raw[:].rearrange("p n j m -> p n (j m)"),
+            in_=key_obj.rearrange("n (p j) m -> p n (j m)", j=PACK),
+        )
+        for c in range(2, CHUNKS):
+            load_h(c, False)
+
+        warm = const.tile([P, 2], F32, name="warm")
+        nc.vector.memset(warm[:], 0.0)
+        nc.scalar.activation(out=warm[:, 1:2], in_=warm[:, 0:1], func=ACT.Exp)
+        ident = const.tile([P, P], F32, name="ident")
+        make_identity(nc, ident[:])
+
+        hg = {}
+        hq = {}
+        ybank = {}
+        qc = {}
+        qg = {}
+        qq = {}
+        simb = {}
+        stat = {}
+        ex = {}
+
+        def h_interleave_scalar(c):
+            t = work.tile([P, CHUNK, PACK], BF16, name="hg", bufs=4, align_bytes=64)
+            nc.scalar.copy(
+                out=t[:, 0:S_SHARE, :].rearrange("p (c i) j -> p c j i", i=RUN),
+                in_=h_view[c][0].rearrange("p j (c i) -> p c j i", i=RUN),
+            )
+            hg[c] = t
+
+        def h_interleave_vector(c):
+            nc.vector.tensor_copy(
+                out=hg[c][:, S_SHARE:CHUNK, :].rearrange("p (c i) j -> p c j i", i=RUN),
+                in_=h_view[c][1].rearrange("p j (c i) -> p c j i", i=RUN),
+            )
+
+        def h_quantize(c):
+            codes = work.tile([P, CHUNK], U32, name="hcodes", bufs=8, align_bytes=64)
+            scales = work.tile([P, CHUNK], U8, name="hscales", bufs=8, align_bytes=64)
+            nc.vector.quantize_mx(
+                out=codes[:].bitcast(FP8X4),
+                scales=scales[:],
+                in_=hg[c][:].rearrange("p w j -> p (w j)"),
+            )
+            hq[c] = (codes, scales)
+
+        def stage1(c):
+            codes, scales = hq[c]
+            banks = []
+            for t in range(PACK):
+                y = psy.tile([P, CHUNK], BANK_DT, name="y")
+                cols = slice(t * P, (t + 1) * P)
+                nc.tensor.matmul_mx(
+                    out=y[:],
+                    lhsT=w_codes[:, cols].bitcast(FP8X4),
+                    lhsT_scale=w_scales[:, cols],
+                    rhs=codes[:].bitcast(FP8X4),
+                    rhs_scale=scales[:],
+                    start=True,
+                    stop=True,
+                )
+                banks.append(y)
+            ybank[c] = banks
+
+        def evacuate(u):
+            c, i0, i1 = UNITS[u]
+            t_q = work.tile([P, PACK, (i1 - i0) * P], BF16, name="qc", bufs=4)
+            for t in range(PACK):
+                nc.scalar.activation(
+                    out=t_q[:, t, :],
+                    in_=ybank[c][t][:, i0 * P : i1 * P],
+                    func=ACT.Relu,
+                    bias=bias[:, t : t + 1],
+                    scale=gain[:, t : t + 1],
+                )
+            qc[u] = t_q
+
+        def q_interleave(u):
+            c, i0, i1 = UNITS[u]
+            t = work.tile([P, (i1 - i0) * P, PACK], BF16, name="qg", bufs=3, align_bytes=64)
+            nc.vector.tensor_copy(
+                out=t[:].rearrange("p (c i) t -> p c t i", i=RUN),
+                in_=qc[u][:].rearrange("p t (c i) -> p c t i", i=RUN),
+            )
+            qg[u] = t
+
+        def q_quantize(u):
+            c, i0, i1 = UNITS[u]
+            codes = work.tile([P, (i1 - i0) * P], U32, name="qcodes", bufs=3, align_bytes=64)
+            scales = work.tile([P, (i1 - i0) * P], U8, name="qscales", bufs=3, align_bytes=64)
+            nc.vector.quantize_mx(
+                out=codes[:].bitcast(FP8X4),
+                scales=scales[:],
+                in_=qg[u][:].rearrange("p w t -> p (w t)"),
+            )
+            qq[u] = (codes, scales)
+
+        def stage2(u):
+            c, i0, i1 = UNITS[u]
+            n = c // PER_IMAGE
+            codes, scales = qq[u]
+            s_t = pss.tile([P, i1 - i0, REGIONS], F32, name="sim", tag="sim")
+            kcols = slice(n * REGIONS, (n + 1) * REGIONS)
+            for i in range(i1 - i0):
+                cols = slice(i * P, (i + 1) * P)
+                nc.tensor.matmul_mx(
+                    out=s_t[:, i, :],
+                    lhsT=codes[:, cols].bitcast(FP8X4),
+                    lhsT_scale=scales[:, cols],
+                    rhs=k_codes[:, kcols].bitcast(FP8X4),
+                    rhs_scale=k_scales[:, kcols],
+                    start=True,
+                    stop=True,
+                )
+            simb[u] = s_t
+
+        def row_max(u):
+            c, i0, i1 = UNITS[u]
+            mx = work.tile([P, i1 - i0], F32, name="mx", bufs=3)
+            nc.vector.tensor_reduce(out=mx[:], in_=simb[u][:], axis=AX.X, op=ALU.max)
+            stat[(u, "mx")] = mx
+
+        def exponent(u):
+            c, i0, i1 = UNITS[u]
+            nb = work.tile([P, i1 - i0], F32, name="nb", bufs=3)
+            sm = work.tile([P, i1 - i0], F32, name="sm", bufs=3)
+            nc.scalar.activation(out=nb[:], in_=stat[(u, "mx")][:], func=ACT.Copy, scale=-SIM_SCALE)
+            e = work.tile([P, i1 - i0, REGIONS], F32, name="e", bufs=3)
+            for i in range(i1 - i0):
+                nc.scalar.activation(
+                    out=e[:, i, :],
+                    in_=simb[u][:, i, :],
+                    func=ACT.Exp,
+                    bias=nb[:, i : i + 1],
+                    scale=SIM_SCALE,
+                    accum_out=sm[:, i : i + 1],
+                )
+            ex[u] = e
+            stat[(u, "sm")] = sm
+
+        def reciprocal(u):
+            c, i0, i1 = UNITS[u]
+            rc = work.tile([P, i1 - i0], F32, name="rc", bufs=3)
+            nc.vector.reciprocal(out=rc[:], in_=stat[(u, "sm")][:])
+            stat[(u, "rc")] = rc
+
+        def normalise_store(u):
+            c, i0, i1 = UNITS[u]
+            n, w0 = c // PER_IMAGE, (c % PER_IMAGE) * CHUNK
+            rc = stat[(u, "rc")]
+            o = work.tile([P, i1 - i0, REGIONS], F32, name="o", bufs=3)
+            for i in range(i1 - i0):
+                nc.vector.tensor_scalar(
+                    out=o[:, i, :],
+                    in0=ex[u][:, i, :],
+                    scalar1=rc[:, i : i + 1],
+                    scalar2=None,
+                    op0=ALU.mult,
+                )
+            nc.sync.dma_start(
+                out=out[n, w0 + i0 * P : w0 + i1 * P, :].rearrange("(i p) m -> p i m", p=P), in_=o[:]
+            )
+
+        h_interleave_scalar(0)
+        h_interleave_vector(0)
+        w_grouped = const.tile([P, PACK * P * PACK], BF16, name="w_grouped", align_bytes=64)
+        w_words = w_grouped[:].bitcast(F32).rearrange("p (t m u) -> p t m u", t=PACK, u=2)
+        for half in range(2):
+            wT = pss.tile([P, 2, 2, P], F32, name="wT", tag="sim")
+            for tt in range(2):
+                words = w_sb[:, 2 * half + tt, :].bitcast(F32)
+                for u in range(2):
+                    nc.tensor.transpose(wT[:, tt, u, :], words[:, u::2], ident[:])
+            dst = w_words[:, 2 * half : 2 * half + 2, :, :]
+            src = wT[:].rearrange("p t u m -> p t m u")
+            if half == 0:
+                nc.scalar.copy(out=dst, in_=src)
+            else:
+                nc.vector.tensor_copy(out=dst, in_=src)
+        gain = const.tile([P, PACK], F32, name="gain")
+        bias = const.tile([P, PACK], F32, name="bias")
+        nc.vector.tensor_copy(out=gain[:], in_=gain_raw[:])
+        nc.vector.tensor_copy(out=bias[:], in_=bias_raw[:])
+        w_codes = const.tile([P, PACK * P], U32, name="w_codes", align_bytes=64)
+        w_scales = const.tile([P, PACK * P], U8, name="w_scales", align_bytes=64)
+        nc.vector.quantize_mx(out=w_codes[:].bitcast(FP8X4), scales=w_scales[:], in_=w_grouped[:])
+        k_grouped = const.tile([P, IMAGES, REGIONS, PACK], BF16, name="k_grouped", align_bytes=64)
+        k_codes = const.tile([P, IMAGES * REGIONS], U32, name="k_codes", align_bytes=64)
+        k_scales = const.tile([P, IMAGES * REGIONS], U8, name="k_scales", align_bytes=64)
+
+        done = -1
+        for k in range(len(UNITS)):
+            c = UNITS[k][0]
+            if c > done:
+                if c > 0:
+                    h_interleave_scalar(c)
+                    h_interleave_vector(c)
+                h_quantize(c)
+                stage1(c)
+                done = c
+            evacuate(k)
+            q_interleave(k)
+            if k == 0:
+                nc.vector.tensor_copy(out=k_grouped[:], in_=k_raw[:].rearrange("p n j m -> p n m j"))
+            q_quantize(k)
+            if k == 0:
+                nc.vector.quantize_mx(
+                    out=k_codes[:].bitcast(FP8X4),
+                    scales=k_scales[:],
+                    in_=k_grouped[:].rearrange("p n m j -> p (n m j)"),
+                )
+            stage2(k)
+            row_max(k)
+            exponent(k)
+            reciprocal(k)
+            normalise_store(k)

@@ -23,7 +23,7 @@ PER_IMAGE = PIXELS // CHUNK
 CHUNKS = IMAGES * PER_IMAGE
 SUB = CHUNK // P
 SIM_SCALE = CH ** -0.5
-LEAD = 2
+LEAD_H = 2
 BANK_DT = BF16
 Y_BUFS = 6
 UNITS = [(c, 0, SUB) for c in range(CHUNKS - 1)] + [(CHUNKS - 1, 0, 2), (CHUNKS - 1, 2, 4)]
@@ -115,10 +115,11 @@ def tile_spatialocr_module_pa_kernel(tc, h_pix, wp2, sp2, bp2, key_obj, out):
             codes, scales = hq[c]
             banks = []
             for t in range(PACK):
-                y = psy.tile([P, CHUNK], BANK_DT, name="y")
+                if t % 2 == 0:
+                    y = psy.tile([P, 2, CHUNK], BANK_DT, name="y")
                 cols = slice(t * P, (t + 1) * P)
                 nc.tensor.matmul_mx(
-                    out=y[:],
+                    out=y[:, t % 2, :],
                     lhsT=w_codes[:, cols].bitcast(FP8X4),
                     lhsT_scale=w_scales[:, cols],
                     rhs=codes[:].bitcast(FP8X4),
@@ -126,7 +127,7 @@ def tile_spatialocr_module_pa_kernel(tc, h_pix, wp2, sp2, bp2, key_obj, out):
                     start=True,
                     stop=True,
                 )
-                banks.append(y)
+                banks.append((y, t % 2))
             ybank[c] = banks
 
         def evacuate(u):
@@ -135,7 +136,7 @@ def tile_spatialocr_module_pa_kernel(tc, h_pix, wp2, sp2, bp2, key_obj, out):
             for t in range(PACK):
                 nc.scalar.activation(
                     out=t_q[:, t, :],
-                    in_=ybank[c][t][:, i0 * P : i1 * P],
+                    in_=ybank[c][t][0][:, ybank[c][t][1], i0 * P : i1 * P],
                     func=ACT.Relu,
                     bias=bias[:, t : t + 1],
                     scale=gain[:, t : t + 1],
@@ -228,6 +229,7 @@ def tile_spatialocr_module_pa_kernel(tc, h_pix, wp2, sp2, bp2, key_obj, out):
                 out=out[n, w0 + i0 * P : w0 + i1 * P, :].rearrange("(i p) m -> p i m", p=P), in_=o[:]
             )
 
+        ctx.enter_context(tc.manual_schedule(engines={mybir.EngineType.DVE, mybir.EngineType.Activation}))
         h_interleave_scalar(0)
         h_interleave_vector(0)
         w_grouped = const.tile([P, PACK * P * PACK], BF16, name="w_grouped", align_bytes=64)
@@ -255,29 +257,33 @@ def tile_spatialocr_module_pa_kernel(tc, h_pix, wp2, sp2, bp2, key_obj, out):
         k_codes = const.tile([P, IMAGES * REGIONS], U32, name="k_codes", align_bytes=64)
         k_scales = const.tile([P, IMAGES * REGIONS], U8, name="k_scales", align_bytes=64)
 
-        done = -1
-        for k in range(len(UNITS)):
-            c = UNITS[k][0]
-            if c > done:
-                if c > 0:
-                    h_interleave_scalar(c)
-                    h_interleave_vector(c)
-                h_quantize(c)
-                stage1(c)
-                done = c
-            evacuate(k)
-            q_interleave(k)
-            if k == 0:
+        n_units = len(UNITS)
+        for i in range(-LEAD_H, n_units + 2):
+            if 0 <= i < n_units:
+                q_interleave(i)
+            if i == -1:
                 nc.vector.tensor_copy(out=k_grouped[:], in_=k_raw[:].rearrange("p n j m -> p n m j"))
-            q_quantize(k)
-            if k == 0:
+            if 0 <= i + LEAD_H < CHUNKS:
+                h_quantize(i + LEAD_H)
+                stage1(i + LEAD_H)
+            if 0 <= i + 1 < n_units:
+                evacuate(i + 1)
+            if 0 <= i - 1 < n_units:
+                row_max(i - 1)
+                exponent(i - 1)
+            if 0 <= i < n_units:
+                q_quantize(i)
+            if i == 0:
                 nc.vector.quantize_mx(
                     out=k_codes[:].bitcast(FP8X4),
                     scales=k_scales[:],
                     in_=k_grouped[:].rearrange("p n m j -> p (n m j)"),
                 )
-            stage2(k)
-            row_max(k)
-            exponent(k)
-            reciprocal(k)
-            normalise_store(k)
+            if 0 <= i < n_units:
+                stage2(i)
+            if 0 <= i + LEAD_H + 1 < CHUNKS:
+                h_interleave_scalar(i + LEAD_H + 1)
+                h_interleave_vector(i + LEAD_H + 1)
+            if 0 <= i - 2 < n_units:
+                reciprocal(i - 2)
+                normalise_store(i - 2)

@@ -18,12 +18,14 @@ PACK = 4
 CHUNK = 512
 HALF = 256
 RUN = 4
-S_SHARE = 192
+S_SHARE = 224
 PER_IMAGE = PIXELS // CHUNK
 CHUNKS = IMAGES * PER_IMAGE
 SUB = CHUNK // P
 SIM_SCALE = CH ** -0.5
-LEAD_H = 2
+LEAD_Q = 3
+LEAD_I = 5
+W_STEP = -2
 BANK_DT = BF16
 Y_BUFS = 6
 UNITS = [(c, 0, SUB) for c in range(CHUNKS - 1)] + [(CHUNKS - 1, 0, 2), (CHUNKS - 1, 2, 4)]
@@ -60,15 +62,17 @@ def tile_spatialocr_module_pa_kernel(tc, h_pix, wp2, sp2, bp2, key_obj, out):
         nc.scalar.dma_start(out=gain_raw[:], in_=sp2.rearrange("(p t) -> p t", t=PACK))
         nc.scalar.dma_start(out=bias_raw[:], in_=bp2.rearrange("(p t) -> p t", t=PACK))
         load_h(0, True)
+        load_h(1, False)
         w_sb = const.tile([P, PACK, CH], BF16, name="w_sb")
         nc.sync.dma_start(out=w_sb[:], in_=wp2.rearrange("(m t) k -> m t k", t=PACK))
-        load_h(1, False)
+        load_h(2, False)
+        load_h(3, False)
         k_raw = const.tile([P, IMAGES, PACK, REGIONS], BF16, name="k_raw")
         nc.sync.dma_start(
             out=k_raw[:].rearrange("p n j m -> p n (j m)"),
             in_=key_obj.rearrange("n (p j) m -> p n (j m)", j=PACK),
         )
-        for c in range(2, CHUNKS):
+        for c in range(4, CHUNKS):
             load_h(c, False)
 
         warm = const.tile([P, 2], F32, name="warm")
@@ -88,14 +92,14 @@ def tile_spatialocr_module_pa_kernel(tc, h_pix, wp2, sp2, bp2, key_obj, out):
         ex = {}
 
         def h_interleave_scalar(c):
-            t = work.tile([P, CHUNK, PACK], BF16, name="hg", bufs=4, align_bytes=64)
+            t = hg[c]
             nc.scalar.copy(
                 out=t[:, 0:S_SHARE, :].rearrange("p (c i) j -> p c j i", i=RUN),
                 in_=h_view[c][0].rearrange("p j (c i) -> p c j i", i=RUN),
             )
-            hg[c] = t
 
         def h_interleave_vector(c):
+            hg[c] = work.tile([P, CHUNK, PACK], BF16, name="hg", bufs=4, align_bytes=64)
             nc.vector.tensor_copy(
                 out=hg[c][:, S_SHARE:CHUNK, :].rearrange("p (c i) j -> p c j i", i=RUN),
                 in_=h_view[c][1].rearrange("p j (c i) -> p c j i", i=RUN),
@@ -230,42 +234,46 @@ def tile_spatialocr_module_pa_kernel(tc, h_pix, wp2, sp2, bp2, key_obj, out):
             )
 
         ctx.enter_context(tc.manual_schedule(engines={mybir.EngineType.DVE, mybir.EngineType.Activation}))
-        h_interleave_scalar(0)
-        h_interleave_vector(0)
         w_grouped = const.tile([P, PACK * P * PACK], BF16, name="w_grouped", align_bytes=64)
         w_words = w_grouped[:].bitcast(F32).rearrange("p (t m u) -> p t m u", t=PACK, u=2)
-        for half in range(2):
-            wT = pss.tile([P, 2, 2, P], F32, name="wT", tag="sim")
-            for tt in range(2):
-                words = w_sb[:, 2 * half + tt, :].bitcast(F32)
-                for u in range(2):
-                    nc.tensor.transpose(wT[:, tt, u, :], words[:, u::2], ident[:])
-            dst = w_words[:, 2 * half : 2 * half + 2, :, :]
-            src = wT[:].rearrange("p t u m -> p t m u")
-            if half == 0:
-                nc.scalar.copy(out=dst, in_=src)
-            else:
-                nc.vector.tensor_copy(out=dst, in_=src)
         gain = const.tile([P, PACK], F32, name="gain")
         bias = const.tile([P, PACK], F32, name="bias")
-        nc.vector.tensor_copy(out=gain[:], in_=gain_raw[:])
-        nc.vector.tensor_copy(out=bias[:], in_=bias_raw[:])
         w_codes = const.tile([P, PACK * P], U32, name="w_codes", align_bytes=64)
         w_scales = const.tile([P, PACK * P], U8, name="w_scales", align_bytes=64)
-        nc.vector.quantize_mx(out=w_codes[:].bitcast(FP8X4), scales=w_scales[:], in_=w_grouped[:])
         k_grouped = const.tile([P, IMAGES, REGIONS, PACK], BF16, name="k_grouped", align_bytes=64)
         k_codes = const.tile([P, IMAGES * REGIONS], U32, name="k_codes", align_bytes=64)
         k_scales = const.tile([P, IMAGES * REGIONS], U8, name="k_scales", align_bytes=64)
 
+        def weights_turn():
+            for half in range(2):
+                wT = pss.tile([P, 2, 2, P], F32, name="wT", tag="sim")
+                for tt in range(2):
+                    words = w_sb[:, 2 * half + tt, :].bitcast(F32)
+                    for u in range(2):
+                        nc.tensor.transpose(wT[:, tt, u, :], words[:, u::2], ident[:])
+                dst = w_words[:, 2 * half : 2 * half + 2, :, :]
+                src = wT[:].rearrange("p t u m -> p t m u")
+                if half == 0:
+                    nc.scalar.copy(out=dst, in_=src)
+                else:
+                    nc.vector.tensor_copy(out=dst, in_=src)
+            nc.vector.tensor_copy(out=gain[:], in_=gain_raw[:])
+            nc.vector.tensor_copy(out=bias[:], in_=bias_raw[:])
+
         n_units = len(UNITS)
-        for i in range(-LEAD_H, n_units + 2):
+        for i in range(-LEAD_I, n_units + 2):
             if 0 <= i < n_units:
                 q_interleave(i)
             if i == -1:
                 nc.vector.tensor_copy(out=k_grouped[:], in_=k_raw[:].rearrange("p n j m -> p n m j"))
-            if 0 <= i + LEAD_H < CHUNKS:
-                h_quantize(i + LEAD_H)
-                stage1(i + LEAD_H)
+            if 0 <= i + LEAD_Q < CHUNKS:
+                h_quantize(i + LEAD_Q)
+            if i == W_STEP:
+                nc.vector.quantize_mx(out=w_codes[:].bitcast(FP8X4), scales=w_scales[:], in_=w_grouped[:])
+                for c in range(i + LEAD_Q):
+                    stage1(c)
+            if i >= W_STEP and 0 <= i + LEAD_Q < CHUNKS:
+                stage1(i + LEAD_Q)
             if 0 <= i + 1 < n_units:
                 evacuate(i + 1)
             if 0 <= i - 1 < n_units:
@@ -281,9 +289,12 @@ def tile_spatialocr_module_pa_kernel(tc, h_pix, wp2, sp2, bp2, key_obj, out):
                 )
             if 0 <= i < n_units:
                 stage2(i)
-            if 0 <= i + LEAD_H + 1 < CHUNKS:
-                h_interleave_scalar(i + LEAD_H + 1)
-                h_interleave_vector(i + LEAD_H + 1)
+            if 0 <= i + LEAD_I < CHUNKS:
+                h_interleave_vector(i + LEAD_I)
+            if i == W_STEP - 1:
+                weights_turn()
+            if 0 <= i + LEAD_I < CHUNKS:
+                h_interleave_scalar(i + LEAD_I)
             if 0 <= i - 2 < n_units:
                 reciprocal(i - 2)
                 normalise_store(i - 2)

@@ -17,7 +17,7 @@ P = 128
 PACK = 4
 CHUNK = 512
 HALF = 256
-RUN = 4
+RUN = 8
 S_SHARE = 224
 PER_IMAGE = PIXELS // CHUNK
 CHUNKS = IMAGES * PER_IMAGE

@@ -18,7 +18,7 @@ PACK = 4
 CHUNK = 512
 HALF = 256
 RUN = 8
-S_SHARE = 224
+S_SHARE = 192
 PER_IMAGE = PIXELS // CHUNK
 CHUNKS = IMAGES * PER_IMAGE
 SUB = CHUNK // P

@@ -23,8 +23,8 @@ PER_IMAGE = PIXELS // CHUNK
 CHUNKS = IMAGES * PER_IMAGE
 SUB = CHUNK // P
 SIM_SCALE = CH ** -0.5
-LEAD_Q = 3
-LEAD_I = 5
+LEAD_Q = 2
+LEAD_I = 3
 W_STEP = -2
 BANK_DT = BF16
 Y_BUFS = 6
@@ -61,18 +61,16 @@ def tile_spatialocr_module_pa_kernel(tc, h_pix, wp2, sp2, bp2, key_obj, out):
         bias_raw = const.tile([P, PACK], BF16, name="bias_raw")
         nc.scalar.dma_start(out=gain_raw[:], in_=sp2.rearrange("(p t) -> p t", t=PACK))
         nc.scalar.dma_start(out=bias_raw[:], in_=bp2.rearrange("(p t) -> p t", t=PACK))
-        load_h(0, True)
-        load_h(1, False)
         w_sb = const.tile([P, PACK, CH], BF16, name="w_sb")
         nc.sync.dma_start(out=w_sb[:], in_=wp2.rearrange("(m t) k -> m t k", t=PACK))
-        load_h(2, False)
-        load_h(3, False)
+        load_h(0, True)
+        load_h(1, False)
         k_raw = const.tile([P, IMAGES, PACK, REGIONS], BF16, name="k_raw")
         nc.sync.dma_start(
             out=k_raw[:].rearrange("p n j m -> p n (j m)"),
             in_=key_obj.rearrange("n (p j) m -> p n (j m)", j=PACK),
         )
-        for c in range(4, CHUNKS):
+        for c in range(2, CHUNKS):
             load_h(c, False)
 
         warm = const.tile([P, 2], F32, name="warm")
@@ -257,8 +255,8 @@ def tile_spatialocr_module_pa_kernel(tc, h_pix, wp2, sp2, bp2, key_obj, out):
                     nc.scalar.copy(out=dst, in_=src)
                 else:
                     nc.vector.tensor_copy(out=dst, in_=src)
-            nc.vector.tensor_copy(out=gain[:], in_=gain_raw[:])
-            nc.vector.tensor_copy(out=bias[:], in_=bias_raw[:])
+            nc.gpsimd.tensor_copy(out=gain[:], in_=gain_raw[:])
+            nc.gpsimd.tensor_copy(out=bias[:], in_=bias_raw[:])
 
         n_units = len(UNITS)
         for i in range(-LEAD_I, n_units + 2):
@@ -289,11 +287,10 @@ def tile_spatialocr_module_pa_kernel(tc, h_pix, wp2, sp2, bp2, key_obj, out):
                 )
             if 0 <= i < n_units:
                 stage2(i)
-            if 0 <= i + LEAD_I < CHUNKS:
-                h_interleave_vector(i + LEAD_I)
             if i == W_STEP - 1:
                 weights_turn()
             if 0 <= i + LEAD_I < CHUNKS:
+                h_interleave_vector(i + LEAD_I)
                 h_interleave_scalar(i + LEAD_I)
             if 0 <= i - 2 < n_units:
                 reciprocal(i - 2)

@@ -132,10 +132,12 @@ def tile_spatialocr_module_pa_kernel(tc, h_pix, wp2, sp2, bp2, key_obj, out):
                 banks.append((y, t % 2))
             ybank[c] = banks
 
-        def evacuate(u):
+        def evacuate(u, slots):
             c, i0, i1 = UNITS[u]
-            t_q = work.tile([P, PACK, (i1 - i0) * P], BF16, name="qc", bufs=4)
-            for t in range(PACK):
+            if u not in qc:
+                qc[u] = work.tile([P, PACK, (i1 - i0) * P], BF16, name="qc", bufs=4)
+            t_q = qc[u]
+            for t in slots:
                 nc.scalar.activation(
                     out=t_q[:, t, :],
                     in_=ybank[c][t][0][:, ybank[c][t][1], i0 * P : i1 * P],
@@ -143,7 +145,6 @@ def tile_spatialocr_module_pa_kernel(tc, h_pix, wp2, sp2, bp2, key_obj, out):
                     bias=bias[:, t : t + 1],
                     scale=gain[:, t : t + 1],
                 )
-            qc[u] = t_q
 
         def q_interleave(u):
             c, i0, i1 = UNITS[u]
@@ -190,11 +191,16 @@ def tile_spatialocr_module_pa_kernel(tc, h_pix, wp2, sp2, bp2, key_obj, out):
             nc.vector.tensor_reduce(out=mx[:], in_=simb[u][:], axis=AX.X, op=ALU.max)
             stat[(u, "mx")] = mx
 
-        def exponent(u):
+        def shift(u):
             c, i0, i1 = UNITS[u]
             nb = work.tile([P, i1 - i0], F32, name="nb", bufs=3)
-            sm = work.tile([P, i1 - i0], F32, name="sm", bufs=3)
             nc.scalar.activation(out=nb[:], in_=stat[(u, "mx")][:], func=ACT.Copy, scale=-SIM_SCALE)
+            stat[(u, "nb")] = nb
+
+        def exponent(u):
+            c, i0, i1 = UNITS[u]
+            nb = stat[(u, "nb")]
+            sm = work.tile([P, i1 - i0], F32, name="sm", bufs=3)
             e = work.tile([P, i1 - i0, REGIONS], F32, name="e", bufs=3)
             for i in range(i1 - i0):
                 nc.scalar.activation(
@@ -262,20 +268,25 @@ def tile_spatialocr_module_pa_kernel(tc, h_pix, wp2, sp2, bp2, key_obj, out):
         for i in range(-LEAD_I, n_units + 2):
             if 0 <= i < n_units:
                 q_interleave(i)
+            if 0 <= i - 1 < n_units:
+                row_max(i - 1)
+            if 0 <= i - 2 < n_units:
+                reciprocal(i - 2)
             if i == -1:
                 nc.vector.tensor_copy(out=k_grouped[:], in_=k_raw[:].rearrange("p n j m -> p n m j"))
-            if 0 <= i + LEAD_Q < CHUNKS:
-                h_quantize(i + LEAD_Q)
             if i == W_STEP:
                 nc.vector.quantize_mx(out=w_codes[:].bitcast(FP8X4), scales=w_scales[:], in_=w_grouped[:])
-                for c in range(i + LEAD_Q):
-                    stage1(c)
+            if 0 <= i + LEAD_Q < CHUNKS:
+                h_quantize(i + LEAD_Q)
             if i >= W_STEP and 0 <= i + LEAD_Q < CHUNKS:
                 stage1(i + LEAD_Q)
             if 0 <= i + 1 < n_units:
-                evacuate(i + 1)
+                evacuate(i + 1, range(PACK - 1))
             if 0 <= i - 1 < n_units:
-                row_max(i - 1)
+                shift(i - 1)
+            if 0 <= i + 1 < n_units:
+                evacuate(i + 1, range(PACK - 1, PACK))
+            if 0 <= i - 1 < n_units:
                 exponent(i - 1)
             if 0 <= i < n_units:
                 q_quantize(i)
@@ -293,5 +304,4 @@ def tile_spatialocr_module_pa_kernel(tc, h_pix, wp2, sp2, bp2, key_obj, out):
                 h_interleave_vector(i + LEAD_I)
                 h_interleave_scalar(i + LEAD_I)
             if 0 <= i - 2 < n_units:
-                reciprocal(i - 2)
                 normalise_store(i - 2)

@@ -19,6 +19,9 @@ CHUNK = 512
 HALF = 256
 RUN = 8
 S_SHARE = 192
+FIRST_T = 2
+T_PART = 256
+S_PART = 64
 PER_IMAGE = PIXELS // CHUNK
 CHUNKS = IMAGES * PER_IMAGE
 SUB = CHUNK // P
@@ -27,7 +30,7 @@ LEAD_Q = 2
 LEAD_I = 3
 W_STEP = -2
 BANK_DT = BF16
-Y_BUFS = 6
+Y_BUFS = 4
 UNITS = [(c, 0, SUB) for c in range(CHUNKS - 1)] + [(CHUNKS - 1, 0, 2), (CHUNKS - 1, 2, 4)]
 
 FLOPS = 2 * IMAGES * CH * CH * PIXELS + 2 * IMAGES * PIXELS * CH * REGIONS
@@ -40,6 +43,7 @@ def tile_spatialocr_module_pa_kernel(tc, h_pix, wp2, sp2, bp2, key_obj, out):
         work = ctx.enter_context(tc.tile_pool(name="work", bufs=2))
         psy = ctx.enter_context(tc.psum_pool(name="psy", bufs=Y_BUFS))
         pss = ctx.enter_context(tc.psum_pool(name="pss", bufs=2))
+        psh = ctx.enter_context(tc.psum_pool(name="psh", bufs=2))
 
         h_view = {}
 
@@ -55,7 +59,9 @@ def tile_spatialocr_module_pa_kernel(tc, h_pix, wp2, sp2, bp2, key_obj, out):
             else:
                 t = const.tile([P, PACK, CHUNK], BF16, name="h%d" % c)
                 nc.sync.dma_start(out=t[:], in_=src[:, :, w0 : w0 + CHUNK])
-                h_view[c] = [t[:, :, 0:S_SHARE], t[:, :, S_SHARE:CHUNK]]
+                first = 0 if c < FIRST_T else T_PART
+                mid = S_SHARE if c < FIRST_T else T_PART + S_PART
+                h_view[c] = [t[:, :, first:mid], t[:, :, mid:CHUNK], t[:, :, 0:T_PART]]
 
         gain_raw = const.tile([P, PACK], BF16, name="gain_raw")
         bias_raw = const.tile([P, PACK], BF16, name="bias_raw")
@@ -78,8 +84,11 @@ def tile_spatialocr_module_pa_kernel(tc, h_pix, wp2, sp2, bp2, key_obj, out):
         nc.scalar.activation(out=warm[:, 1:2], in_=warm[:, 0:1], func=ACT.Exp)
         ident = const.tile([P, P], F32, name="ident")
         make_identity(nc, ident[:])
+        ident_bf = const.tile([P, P], BF16, name="ident_bf")
+        make_identity(nc, ident_bf[:])
 
         hg = {}
+        hbank = {}
         hq = {}
         ybank = {}
         qc = {}
@@ -89,17 +98,35 @@ def tile_spatialocr_module_pa_kernel(tc, h_pix, wp2, sp2, bp2, key_obj, out):
         stat = {}
         ex = {}
 
+        def h_interleave_tensor(c):
+            b = psh.tile([P, T_PART, PACK], BF16, name="hbank")
+            for k in range(T_PART // P):
+                cols = slice(k * P, (k + 1) * P)
+                nc.tensor.matmul(
+                    out=b[:, cols, :],
+                    lhsT=ident_bf[:],
+                    rhs=h_view[c][2][:, :, cols].rearrange("p j w -> p w j"),
+                    start=True,
+                    stop=True,
+                )
+            hbank[c] = b
+
         def h_interleave_scalar(c):
             t = hg[c]
+            first = 0 if c < FIRST_T else T_PART
+            mid = S_SHARE if c < FIRST_T else T_PART + S_PART
+            if c >= FIRST_T:
+                nc.scalar.copy(out=t[:, 0:T_PART, :], in_=hbank[c][:])
             nc.scalar.copy(
-                out=t[:, 0:S_SHARE, :].rearrange("p (c i) j -> p c j i", i=RUN),
+                out=t[:, first:mid, :].rearrange("p (c i) j -> p c j i", i=RUN),
                 in_=h_view[c][0].rearrange("p j (c i) -> p c j i", i=RUN),
             )
 
         def h_interleave_vector(c):
+            mid = S_SHARE if c < FIRST_T else T_PART + S_PART
             hg[c] = work.tile([P, CHUNK, PACK], BF16, name="hg", bufs=4, align_bytes=64)
             nc.vector.tensor_copy(
-                out=hg[c][:, S_SHARE:CHUNK, :].rearrange("p (c i) j -> p c j i", i=RUN),
+                out=hg[c][:, mid:CHUNK, :].rearrange("p (c i) j -> p c j i", i=RUN),
                 in_=h_view[c][1].rearrange("p j (c i) -> p c j i", i=RUN),
             )
 
@@ -237,7 +264,7 @@ def tile_spatialocr_module_pa_kernel(tc, h_pix, wp2, sp2, bp2, key_obj, out):
                 out=out[n, w0 + i0 * P : w0 + i1 * P, :].rearrange("(i p) m -> p i m", p=P), in_=o[:]
             )
 
-        ctx.enter_context(tc.manual_schedule(engines={mybir.EngineType.DVE, mybir.EngineType.Activation}))
+        ctx.enter_context(tc.manual_schedule(engines={mybir.EngineType.DVE, mybir.EngineType.Activation, mybir.EngineType.PE}))
         w_grouped = const.tile([P, PACK * P * PACK], BF16, name="w_grouped", align_bytes=64)
         w_words = w_grouped[:].bitcast(F32).rearrange("p (t m u) -> p t m u", t=PACK, u=2)
         gain = const.tile([P, PACK], F32, name="gain")
@@ -303,5 +330,7 @@ def tile_spatialocr_module_pa_kernel(tc, h_pix, wp2, sp2, bp2, key_obj, out):
             if 0 <= i + LEAD_I < CHUNKS:
                 h_interleave_vector(i + LEAD_I)
                 h_interleave_scalar(i + LEAD_I)
+            if FIRST_T <= i + LEAD_I + 1 < CHUNKS:
+                h_interleave_tensor(i + LEAD_I + 1)
             if 0 <= i - 2 < n_units:
                 normalise_store(i - 2)

@@ -21,7 +21,7 @@ RUN = 8
 S_SHARE = 192
 FIRST_T = 2
 T_PART = 256
-S_PART = 64
+S_PART = 32
 PER_IMAGE = PIXELS // CHUNK
 CHUNKS = IMAGES * PER_IMAGE
 SUB = CHUNK // P

@@ -31,6 +31,8 @@ LEAD_I = 3
 W_STEP = -2
 BANK_DT = BF16
 Y_BUFS = 4
+WARM_A = 3
+WARM_B = 4
 UNITS = [(c, 0, SUB) for c in range(CHUNKS - 1)] + [(CHUNKS - 1, 0, 2), (CHUNKS - 1, 2, 4)]
 
 FLOPS = 2 * IMAGES * CH * CH * PIXELS + 2 * IMAGES * PIXELS * CH * REGIONS
@@ -67,8 +69,13 @@ def tile_spatialocr_module_pa_kernel(tc, h_pix, wp2, sp2, bp2, key_obj, out):
         bias_raw = const.tile([P, PACK], BF16, name="bias_raw")
         nc.scalar.dma_start(out=gain_raw[:], in_=sp2.rearrange("(p t) -> p t", t=PACK))
         nc.scalar.dma_start(out=bias_raw[:], in_=bp2.rearrange("(p t) -> p t", t=PACK))
-        w_sb = const.tile([P, PACK, CH], BF16, name="w_sb")
-        nc.sync.dma_start(out=w_sb[:], in_=wp2.rearrange("(m t) k -> m t k", t=PACK))
+        w_raw = []
+        for half in range(2):
+            t_w = const.tile([P, 2, CH], BF16, name="w_raw%d" % half)
+            nc.sync.dma_start(
+                out=t_w[:], in_=wp2.rearrange("(m t) k -> m t k", t=PACK)[:, 2 * half : 2 * half + 2, :]
+            )
+            w_raw.append(t_w)
         load_h(0, True)
         load_h(1, False)
         k_raw = const.tile([P, IMAGES, PACK, REGIONS], BF16, name="k_raw")
@@ -279,7 +286,7 @@ def tile_spatialocr_module_pa_kernel(tc, h_pix, wp2, sp2, bp2, key_obj, out):
             for half in range(2):
                 wT = pss.tile([P, 2, 2, P], F32, name="wT", tag="sim")
                 for tt in range(2):
-                    words = w_sb[:, 2 * half + tt, :].bitcast(F32)
+                    words = w_raw[half][:, tt, :].bitcast(F32)
                     for u in range(2):
                         nc.tensor.transpose(wT[:, tt, u, :], words[:, u::2], ident[:])
                 dst = w_words[:, 2 * half : 2 * half + 2, :, :]
@@ -290,6 +297,11 @@ def tile_spatialocr_module_pa_kernel(tc, h_pix, wp2, sp2, bp2, key_obj, out):
                     nc.vector.tensor_copy(out=dst, in_=src)
             nc.gpsimd.tensor_copy(out=gain[:], in_=gain_raw[:])
             nc.gpsimd.tensor_copy(out=bias[:], in_=bias_raw[:])
+
+        def warm_up(moving, count):
+            t = psh.tile([P, P], F32, name="hbank")
+            for k in range(count):
+                nc.tensor.matmul(out=t[:], lhsT=ident[:], rhs=moving, start=True, stop=True)
 
         n_units = len(UNITS)
         for i in range(-LEAD_I, n_units + 2):
@@ -326,7 +338,9 @@ def tile_spatialocr_module_pa_kernel(tc, h_pix, wp2, sp2, bp2, key_obj, out):
             if 0 <= i < n_units:
                 stage2(i)
             if i == W_STEP - 1:
+                warm_up(ident[:], WARM_A)
                 weights_turn()
+                warm_up(w_grouped[:].bitcast(F32)[:, 0:P], WARM_B)
             if 0 <= i + LEAD_I < CHUNKS:
                 h_interleave_vector(i + LEAD_I)
                 h_interleave_scalar(i + LEAD_I)

@@ -118,8 +118,13 @@ def tile_spatialocr_module_pa_kernel(tc, h_pix, wp2, sp2, bp2, key_obj, out):
                 )
             hbank[c] = b
 
+        def h_grouped(c):
+            if c not in hg:
+                hg[c] = work.tile([P, CHUNK, PACK], BF16, name="hg", bufs=4, align_bytes=64)
+            return hg[c]
+
         def h_interleave_scalar(c):
-            t = hg[c]
+            t = h_grouped(c)
             first = 0 if c < FIRST_T else T_PART
             mid = S_SHARE if c < FIRST_T else T_PART + S_PART
             if c >= FIRST_T:
@@ -131,9 +136,8 @@ def tile_spatialocr_module_pa_kernel(tc, h_pix, wp2, sp2, bp2, key_obj, out):
 
         def h_interleave_vector(c):
             mid = S_SHARE if c < FIRST_T else T_PART + S_PART
-            hg[c] = work.tile([P, CHUNK, PACK], BF16, name="hg", bufs=4, align_bytes=64)
             nc.vector.tensor_copy(
-                out=hg[c][:, mid:CHUNK, :].rearrange("p (c i) j -> p c j i", i=RUN),
+                out=h_grouped(c)[:, mid:CHUNK, :].rearrange("p (c i) j -> p c j i", i=RUN),
                 in_=h_view[c][1].rearrange("p j (c i) -> p c j i", i=RUN),
             )
 
@@ -320,11 +324,11 @@ def tile_spatialocr_module_pa_kernel(tc, h_pix, wp2, sp2, bp2, key_obj, out):
             if i >= W_STEP and 0 <= i + LEAD_Q < CHUNKS:
                 stage1(i + LEAD_Q)
             if 0 <= i + 1 < n_units:
-                evacuate(i + 1, range(PACK - 1))
+                evacuate(i + 1, range(PACK))
             if 0 <= i - 1 < n_units:
                 shift(i - 1)
-            if 0 <= i + 1 < n_units:
-                evacuate(i + 1, range(PACK - 1, PACK))
+            if 0 <= i and i + LEAD_I < CHUNKS:
+                h_interleave_scalar(i + LEAD_I)
             if 0 <= i - 1 < n_units:
                 exponent(i - 1)
             if 0 <= i < n_units:
@@ -343,6 +347,7 @@ def tile_spatialocr_module_pa_kernel(tc, h_pix, wp2, sp2, bp2, key_obj, out):
                 warm_up(w_grouped[:].bitcast(F32)[:, 0:P], WARM_B)
             if 0 <= i + LEAD_I < CHUNKS:
                 h_interleave_vector(i + LEAD_I)
+            if i < 0 and 0 <= i + LEAD_I:
                 h_interleave_scalar(i + LEAD_I)
             if FIRST_T <= i + LEAD_I + 1 < CHUNKS:
                 h_interleave_tensor(i + LEAD_I + 1)

from contextlib import ExitStack

import concourse.mybir as mybir
from concourse.masks import make_identity

F32 = mybir.dt.float32
BF16 = mybir.dt.bfloat16
U32 = mybir.dt.uint32
U8 = mybir.dt.uint8
FP8X4 = mybir.dt.float8_e4m3fn_x4
ACT = mybir.ActivationFunctionType
ALU = mybir.AluOpType
AX = mybir.AxisListType

IMAGES, CH, PIXELS, REGIONS = 4, 512, 1024, 128
P = 128
PACK = 4
CHUNK = 512
HALF = 256
RUN = 8
S_SHARE = 192
FIRST_T = 2
T_PART = 256
S_PART = 32
PER_IMAGE = PIXELS // CHUNK
CHUNKS = IMAGES * PER_IMAGE
SUB = CHUNK // P
SIM_SCALE = CH ** -0.5
LEAD_Q = 2
LEAD_I = 3
W_STEP = -2
BANK_DT = BF16
Y_BUFS = 4
WARM_A = 3
WARM_B = 4
UNITS = [(c, 0, SUB) for c in range(CHUNKS - 1)] + [(CHUNKS - 1, 0, 2), (CHUNKS - 1, 2, 4)]

FLOPS = 2 * IMAGES * CH * CH * PIXELS + 2 * IMAGES * PIXELS * CH * REGIONS


def tile_spatialocr_module_pa_kernel(tc, h_pix, wp2, sp2, bp2, key_obj, out):
    nc = tc.nc
    with ExitStack() as ctx:
        const = ctx.enter_context(tc.tile_pool(name="const", bufs=1))
        work = ctx.enter_context(tc.tile_pool(name="work", bufs=2))
        psy = ctx.enter_context(tc.psum_pool(name="psy", bufs=Y_BUFS))
        pss = ctx.enter_context(tc.psum_pool(name="pss", bufs=2))
        psh = ctx.enter_context(tc.psum_pool(name="psh", bufs=2))

        h_view = {}

        def load_h(c, split):
            n, w0 = c // PER_IMAGE, (c % PER_IMAGE) * CHUNK
            src = h_pix[n].rearrange("(p j) w -> p j w", j=PACK)
            if split:
                t_s = const.tile([P, PACK, S_SHARE], BF16, name="h%d_s" % c)
                t_v = const.tile([P, PACK, CHUNK - S_SHARE], BF16, name="h%d_v" % c)
                nc.sync.dma_start(out=t_v[:], in_=src[:, :, w0 + S_SHARE : w0 + CHUNK])
                nc.sync.dma_start(out=t_s[:], in_=src[:, :, w0 : w0 + S_SHARE])
                h_view[c] = [t_s[:], t_v[:]]
            else:
                t = const.tile([P, PACK, CHUNK], BF16, name="h%d" % c)
                nc.sync.dma_start(out=t[:], in_=src[:, :, w0 : w0 + CHUNK])
                first = 0 if c < FIRST_T else T_PART
                mid = S_SHARE if c < FIRST_T else T_PART + S_PART
                h_view[c] = [t[:, :, first:mid], t[:, :, mid:CHUNK], t[:, :, 0:T_PART]]

        gain_raw = const.tile([P, PACK], BF16, name="gain_raw")
        bias_raw = const.tile([P, PACK], BF16, name="bias_raw")
        nc.scalar.dma_start(out=gain_raw[:], in_=sp2.rearrange("(p t) -> p t", t=PACK))
        nc.scalar.dma_start(out=bias_raw[:], in_=bp2.rearrange("(p t) -> p t", t=PACK))
        w_raw = []
        for half in range(2):
            t_w = const.tile([P, 2, CH], BF16, name="w_raw%d" % half)
            nc.sync.dma_start(
                out=t_w[:], in_=wp2.rearrange("(m t) k -> m t k", t=PACK)[:, 2 * half : 2 * half + 2, :]
            )
            w_raw.append(t_w)
        load_h(0, True)
        load_h(1, False)
        k_raw = const.tile([P, IMAGES, PACK, REGIONS], BF16, name="k_raw")
        nc.sync.dma_start(
            out=k_raw[:].rearrange("p n j m -> p n (j m)"),
            in_=key_obj.rearrange("n (p j) m -> p n (j m)", j=PACK),
        )
        for c in range(2, CHUNKS):
            load_h(c, False)

        warm = const.tile([P, 2], F32, name="warm")
        nc.vector.memset(warm[:], 0.0)
        nc.scalar.activation(out=warm[:, 1:2], in_=warm[:, 0:1], func=ACT.Exp)
        ident = const.tile([P, P], F32, name="ident")
        make_identity(nc, ident[:])
        ident_bf = const.tile([P, P], BF16, name="ident_bf")
        make_identity(nc, ident_bf[:])

        hg = {}
        hbank = {}
        hq = {}
        ybank = {}
        qc = {}
        qg = {}
        qq = {}
        simb = {}
        stat = {}
        ex = {}

        def h_interleave_tensor(c):
            b = psh.tile([P, T_PART, PACK], BF16, name="hbank")
            for k in range(T_PART // P):
                cols = slice(k * P, (k + 1) * P)
                nc.tensor.matmul(
                    out=b[:, cols, :],
                    lhsT=ident_bf[:],
                    rhs=h_view[c][2][:, :, cols].rearrange("p j w -> p w j"),
                    start=True,
                    stop=True,
                )
            hbank[c] = b

        def h_grouped(c):
            if c not in hg:
                hg[c] = work.tile([P, CHUNK, PACK], BF16, name="hg", bufs=4, align_bytes=64)
            return hg[c]

        def h_interleave_scalar(c):
            t = h_grouped(c)
            first = 0 if c < FIRST_T else T_PART
            mid = S_SHARE if c < FIRST_T else T_PART + S_PART
            if c >= FIRST_T:
                nc.scalar.copy(out=t[:, 0:T_PART, :], in_=hbank[c][:])
            nc.scalar.copy(
                out=t[:, first:mid, :].rearrange("p (c i) j -> p c j i", i=RUN),
                in_=h_view[c][0].rearrange("p j (c i) -> p c j i", i=RUN),
            )

        def h_interleave_vector(c):
            mid = S_SHARE if c < FIRST_T else T_PART + S_PART
            nc.vector.tensor_copy(
                out=h_grouped(c)[:, mid:CHUNK, :].rearrange("p (c i) j -> p c j i", i=RUN),
                in_=h_view[c][1].rearrange("p j (c i) -> p c j i", i=RUN),
            )

        def h_quantize(c):
            codes = work.tile([P, CHUNK], U32, name="hcodes", bufs=8, align_bytes=64)
            scales = work.tile([P, CHUNK], U8, name="hscales", bufs=8, align_bytes=64)
            nc.vector.quantize_mx(
                out=codes[:].bitcast(FP8X4),
                scales=scales[:],
                in_=hg[c][:].rearrange("p w j -> p (w j)"),
            )
            hq[c] = (codes, scales)

        def stage1(c):
            codes, scales = hq[c]
            banks = []
            for t in range(PACK):
                if t % 2 == 0:
                    y = psy.tile([P, 2, CHUNK], BANK_DT, name="y")
                cols = slice(t * P, (t + 1) * P)
                nc.tensor.matmul_mx(
                    out=y[:, t % 2, :],
                    lhsT=w_codes[:, cols].bitcast(FP8X4),
                    lhsT_scale=w_scales[:, cols],
                    rhs=codes[:].bitcast(FP8X4),
                    rhs_scale=scales[:],
                    start=True,
                    stop=True,
                )
                banks.append((y, t % 2))
            ybank[c] = banks

        def evacuate(u, slots):
            c, i0, i1 = UNITS[u]
            if u not in qc:
                qc[u] = work.tile([P, PACK, (i1 - i0) * P], BF16, name="qc", bufs=4)
            t_q = qc[u]
            for t in slots:
                nc.scalar.activation(
                    out=t_q[:, t, :],
                    in_=ybank[c][t][0][:, ybank[c][t][1], i0 * P : i1 * P],
                    func=ACT.Relu,
                    bias=bias[:, t : t + 1],
                    scale=gain[:, t : t + 1],
                )

        def q_interleave(u):
            c, i0, i1 = UNITS[u]
            t = work.tile([P, (i1 - i0) * P, PACK], BF16, name="qg", bufs=3, align_bytes=64)
            nc.vector.tensor_copy(
                out=t[:].rearrange("p (c i) t -> p c t i", i=RUN),
                in_=qc[u][:].rearrange("p t (c i) -> p c t i", i=RUN),
            )
            qg[u] = t

        def q_quantize(u):
            c, i0, i1 = UNITS[u]
            codes = work.tile([P, (i1 - i0) * P], U32, name="qcodes", bufs=3, align_bytes=64)
            scales = work.tile([P, (i1 - i0) * P], U8, name="qscales", bufs=3, align_bytes=64)
            nc.vector.quantize_mx(
                out=codes[:].bitcast(FP8X4),
                scales=scales[:],
                in_=qg[u][:].rearrange("p w t -> p (w t)"),
            )
            qq[u] = (codes, scales)

        def stage2(u):
            c, i0, i1 = UNITS[u]
            n = c // PER_IMAGE
            codes, scales = qq[u]
            s_t = pss.tile([P, i1 - i0, REGIONS], F32, name="sim", tag="sim")
            kcols = slice(n * REGIONS, (n + 1) * REGIONS)
            for i in range(i1 - i0):
                cols = slice(i * P, (i + 1) * P)
                nc.tensor.matmul_mx(
                    out=s_t[:, i, :],
                    lhsT=codes[:, cols].bitcast(FP8X4),
                    lhsT_scale=scales[:, cols],
                    rhs=k_codes[:, kcols].bitcast(FP8X4),
                    rhs_scale=k_scales[:, kcols],
                    start=True,
                    stop=True,
                )
            simb[u] = s_t

        def row_max(u):
            c, i0, i1 = UNITS[u]
            mx = work.tile([P, i1 - i0], F32, name="mx", bufs=3)
            nc.vector.tensor_reduce(out=mx[:], in_=simb[u][:], axis=AX.X, op=ALU.max)
            stat[(u, "mx")] = mx

        def shift(u):
            c, i0, i1 = UNITS[u]
            nb = work.tile([P, i1 - i0], F32, name="nb", bufs=3)
            nc.scalar.activation(out=nb[:], in_=stat[(u, "mx")][:], func=ACT.Copy, scale=-SIM_SCALE)
            stat[(u, "nb")] = nb

        def exponent(u):
            c, i0, i1 = UNITS[u]
            nb = stat[(u, "nb")]
            sm = work.tile([P, i1 - i0], F32, name="sm", bufs=3)
            e = work.tile([P, i1 - i0, REGIONS], F32, name="e", bufs=3)
            for i in range(i1 - i0):
                nc.scalar.activation(
                    out=e[:, i, :],
                    in_=simb[u][:, i, :],
                    func=ACT.Exp,
                    bias=nb[:, i : i + 1],
                    scale=SIM_SCALE,
                    accum_out=sm[:, i : i + 1],
                )
            ex[u] = e
            stat[(u, "sm")] = sm

        def reciprocal(u):
            c, i0, i1 = UNITS[u]
            rc = work.tile([P, i1 - i0], F32, name="rc", bufs=3)
            nc.vector.reciprocal(out=rc[:], in_=stat[(u, "sm")][:])
            stat[(u, "rc")] = rc

        def normalise_store(u):
            c, i0, i1 = UNITS[u]
            n, w0 = c // PER_IMAGE, (c % PER_IMAGE) * CHUNK
            rc = stat[(u, "rc")]
            o = work.tile([P, i1 - i0, REGIONS], F32, name="o", bufs=3)
            for i in range(i1 - i0):
                nc.vector.tensor_scalar(
                    out=o[:, i, :],
                    in0=ex[u][:, i, :],
                    scalar1=rc[:, i : i + 1],
                    scalar2=None,
                    op0=ALU.mult,
                )
            nc.sync.dma_start(
                out=out[n, w0 + i0 * P : w0 + i1 * P, :].rearrange("(i p) m -> p i m", p=P), in_=o[:]
            )

        ctx.enter_context(tc.manual_schedule(engines={mybir.EngineType.DVE, mybir.EngineType.Activation, mybir.EngineType.PE}))
        w_grouped = const.tile([P, PACK * P * PACK], BF16, name="w_grouped", align_bytes=64)
        w_words = w_grouped[:].bitcast(F32).rearrange("p (t m u) -> p t m u", t=PACK, u=2)
        gain = const.tile([P, PACK], F32, name="gain")
        bias = const.tile([P, PACK], F32, name="bias")
        w_codes = const.tile([P, PACK * P], U32, name="w_codes", align_bytes=64)
        w_scales = const.tile([P, PACK * P], U8, name="w_scales", align_bytes=64)
        k_grouped = const.tile([P, IMAGES, REGIONS, PACK], BF16, name="k_grouped", align_bytes=64)
        k_codes = const.tile([P, IMAGES * REGIONS], U32, name="k_codes", align_bytes=64)
        k_scales = const.tile([P, IMAGES * REGIONS], U8, name="k_scales", align_bytes=64)

        def weights_turn():
            for half in range(2):
                wT = pss.tile([P, 2, 2, P], F32, name="wT", tag="sim")
                for tt in range(2):
                    words = w_raw[half][:, tt, :].bitcast(F32)
                    for u in range(2):
                        nc.tensor.transpose(wT[:, tt, u, :], words[:, u::2], ident[:])
                dst = w_words[:, 2 * half : 2 * half + 2, :, :]
                src = wT[:].rearrange("p t u m -> p t m u")
                if half == 0:
                    nc.scalar.copy(out=dst, in_=src)
                else:
                    nc.vector.tensor_copy(out=dst, in_=src)
            nc.gpsimd.tensor_copy(out=gain[:], in_=gain_raw[:])
            nc.gpsimd.tensor_copy(out=bias[:], in_=bias_raw[:])

        def warm_up(moving, count):
            t = psh.tile([P, P], F32, name="hbank")
            for k in range(count):
                nc.tensor.matmul(out=t[:], lhsT=ident[:], rhs=moving, start=True, stop=True)

        n_units = len(UNITS)
        for i in range(-LEAD_I, n_units + 2):
            if 0 <= i < n_units:
                q_interleave(i)
            if 0 <= i - 1 < n_units:
                row_max(i - 1)
            if 0 <= i - 2 < n_units:
                reciprocal(i - 2)
            if i == -1:
                nc.vector.tensor_copy(out=k_grouped[:], in_=k_raw[:].rearrange("p n j m -> p n m j"))
            if i == W_STEP:
                nc.vector.quantize_mx(out=w_codes[:].bitcast(FP8X4), scales=w_scales[:], in_=w_grouped[:])
            if 0 <= i + LEAD_Q < CHUNKS:
                h_quantize(i + LEAD_Q)
            if i >= W_STEP and 0 <= i + LEAD_Q < CHUNKS:
                stage1(i + LEAD_Q)
            if 0 <= i + 1 < n_units:
                evacuate(i + 1, range(PACK))
            if 0 <= i - 1 < n_units:
                shift(i - 1)
            if 0 <= i and i + LEAD_I < CHUNKS:
                h_interleave_scalar(i + LEAD_I)
            if 0 <= i - 1 < n_units:
                exponent(i - 1)
            if 0 <= i < n_units:
                q_quantize(i)
            if i == 0:
                nc.vector.quantize_mx(
                    out=k_codes[:].bitcast(FP8X4),
                    scales=k_scales[:],
                    in_=k_grouped[:].rearrange("p n m j -> p (n m j)"),
                )
            if 0 <= i < n_units:
                stage2(i)
            if i == W_STEP - 1:
                warm_up(ident[:], WARM_A)
                weights_turn()
                warm_up(w_grouped[:].bitcast(F32)[:, 0:P], WARM_B)
            if 0 <= i + LEAD_I < CHUNKS:
                h_interleave_vector(i + LEAD_I)
            if i < 0 and 0 <= i + LEAD_I:
                h_interleave_scalar(i + LEAD_I)
            if FIRST_T <= i + LEAD_I + 1 < CHUNKS:
                h_interleave_tensor(i + LEAD_I + 1)
            if 0 <= i - 2 < n_units:
                normalise_store(i - 2)
